import numpy as np
import ml_dtypes


def mxq(x, axis, fmt="e4m3"):
    dtype, down = {"e4m3": (ml_dtypes.float8_e4m3fn, 7), "e5m2": (ml_dtypes.float8_e5m2, 14)}[fmt]
    v = np.moveaxis(np.asarray(x, np.float32).astype(ml_dtypes.bfloat16).astype(np.float64), axis, -1)
    blocks = v.reshape(v.shape[:-1] + (-1, 32))
    amax = np.abs(blocks).max(-1, keepdims=True)
    byte = np.maximum(np.where(amax > 0, np.frexp(amax)[1] - 1 + 127, 0) - down, 1)
    scale = np.exp2(byte - 127.0)
    codes = (blocks / scale).astype(np.float32).astype(dtype).astype(np.float64)
    return np.moveaxis((codes * scale).reshape(v.shape), -1, axis)


WIDE = False


def mx_kscale(k):
    if not WIDE:
        return np.ones(k)
    levels = np.array([10, -10, 5, -5, 0])
    a = np.random.permutation(np.resize(levels, k // 512 * 4)).reshape(k // 512, 4)
    idx = np.arange(k)
    return np.exp2(a[idx // 512, idx % 128 // 32])


BF16 = ml_dtypes.bfloat16


def bf(x):
    return np.asarray(x, np.float32).astype(BF16)


def f64(x):
    return np.asarray(x).astype(np.float64)


B, T, D, LAT, H = 2, 2048, 512, 1024, 4
L = LAT // H
SQ = 2.0


def setup_inputs():
    s = mx_kscale(D)
    return {"query": bf(np.random.standard_normal((B, T, D)) * s),
            "wq": bf(np.random.standard_normal((D, LAT)) * SQ / np.sqrt(D) / s[:, None])}


def reference(query, wq):
    Q = mxq(f64(query), 2, "e4m3") @ mxq(f64(wq), 0, "e4m3")
    Q = Q.transpose(1, 0, 2).reshape(T, B, H, L)
    e = np.exp(Q - Q.max(-1, keepdims=True))
    return e / e.sum(-1, keepdims=True)

@@ -1,0 +1,180 @@
+from contextlib import ExitStack
+
+import concourse.mybir as mybir
+from concourse.masks import make_identity
+
+F32 = mybir.dt.float32
+BF16 = mybir.dt.bfloat16
+U32 = mybir.dt.uint32
+U8 = mybir.dt.uint8
+FP8X4 = mybir.dt.float8_e4m3fn_x4
+ALU = mybir.AluOpType
+ACT = mybir.ActivationFunctionType
+
+P = 128
+BATCH = 2
+TOKENS = 2048
+DEPTH = 512
+SLOTS = 1024
+HEADS = 4
+HEAD = SLOTS // HEADS
+BANK = 512
+HALVES = SLOTS // BANK
+ROUNDS = TOKENS // P
+TILES = ROUNDS * BATCH
+WORDS = DEPTH // 2
+GPSIMD_HEADS = 3
+
+FLOPS = 2 * BATCH * TOKENS * DEPTH * SLOTS
+
+
+def tile_latentattention_pb_t_kernel(tc, query, wq, out):
+    nc = tc.nc
+    with ExitStack() as ctx:
+        keep = ctx.enter_context(tc.tile_pool(name="keep", bufs=1))
+        stage = ctx.enter_context(tc.tile_pool(name="stage", bufs=3))
+        small = ctx.enter_context(tc.tile_pool(name="small", bufs=8))
+        results = ctx.enter_context(tc.tile_pool(name="results", bufs=6))
+        psum_t = ctx.enter_context(tc.psum_pool(name="psum_t", bufs=2))
+        psum_q = ctx.enter_context(tc.psum_pool(name="psum_q", bufs=6))
+
+        query_view = query.rearrange("b (p j) d -> p b j d", j=ROUNDS)
+        out_view = out.rearrange("(p j) b h l -> p j b (h l)", j=ROUNDS)
+        wq_view = wq.rearrange("(u q e) c -> q u (e c)", u=2, e=2)
+
+        q_raw = keep.tile([P, BATCH, ROUNDS, DEPTH], BF16)
+        w_raw = keep.tile([P, 4, SLOTS], BF16)
+        nc.sync.dma_start(out=q_raw[:, :, 0:1, :], in_=query_view[:, :, 0:1, :])
+        nc.sync.dma_start(out=w_raw[:].rearrange("p (u e) c -> p u (e c)", u=2), in_=wq_view)
+        first = 1
+        for piece in range(4):
+            nc.sync.dma_start(
+                out=q_raw[:, :, first : 2 * first, :], in_=query_view[:, :, first : 2 * first, :]
+            )
+            first = 2 * first
+
+        ident = keep.tile([P, P], F32)
+        make_identity(nc, ident[:])
+        zero = keep.tile([P, 1], F32)
+        one = keep.tile([P, 1], F32)
+        nc.vector.memset(zero[:], 0.0)
+        nc.scalar.activation(out=one[:], in_=zero[:], func=ACT.Exp)
+
+        q_words = q_raw[:].bitcast(F32)
+        q_codes = keep.tile([P, ROUNDS, BATCH * P], U32, align_bytes=64)
+        q_scales = keep.tile([P, ROUNDS, BATCH * P], U8, align_bytes=64)
+        w_grouped = keep.tile([P, SLOTS, 4], BF16, align_bytes=64)
+        w_codes = keep.tile([P, SLOTS], U32, align_bytes=64)
+        w_scales = keep.tile([P, SLOTS], U8, align_bytes=64)
+
+        def quantise_queries(j):
+            turned = psum_t.tile([P, BATCH, 2, P], F32)
+            for b in range(BATCH):
+                for u in range(2):
+                    nc.tensor.transpose(
+                        turned[:, b, u, :], q_words[:, b, j, u * P : (u + 1) * P], ident[:]
+                    )
+            grouped = stage.tile([P, BATCH, P, 4], BF16, align_bytes=64)
+            nc.scalar.copy(
+                out=grouped[:].bitcast(F32), in_=turned[:].rearrange("p b u r -> p b r u")
+            )
+            nc.vector.quantize_mx(
+                out=q_codes[:, j, :].bitcast(FP8X4),
+                scales=q_scales[:, j, :],
+                in_=grouped[:].rearrange("p b r t -> p (b r t)"),
+            )
+
+        def quantise_weights(half):
+            cols = slice(half * BANK, (half + 1) * BANK)
+            nc.vector.tensor_copy(
+                out=w_grouped[:, cols, :].rearrange("p (c i) t -> p c t i", i=4),
+                in_=w_raw[:, :, cols].rearrange("p t (c i) -> p c t i", i=4),
+            )
+            nc.vector.quantize_mx(
+                out=w_codes[:, cols].bitcast(FP8X4),
+                scales=w_scales[:, cols],
+                in_=w_grouped[:, cols, :].rearrange("p c t -> p (c t)"),
+            )
+
+        scores = {}
+        neg_max = {}
+        sums = {}
+        weights = {}
+
+        def multiply(i):
+            j, b = divmod(i, BATCH)
+            for half in range(HALVES):
+                cols = slice(half * BANK, (half + 1) * BANK)
+                bank = psum_q.tile([P, BANK], F32, name="bank")
+                nc.tensor.matmul_mx(
+                    out=bank[:],
+                    lhsT=q_codes[:, j, b * P : (b + 1) * P].bitcast(FP8X4),
+                    lhsT_scale=q_scales[:, j, b * P : (b + 1) * P],
+                    rhs=w_codes[:, cols].bitcast(FP8X4),
+                    rhs_scale=w_scales[:, cols],
+                    start=True,
+                    stop=True,
+                )
+                scores[(i, half)] = bank
+
+        def exponentials(i):
+            j, b = divmod(i, BATCH)
+            if b == 0:
+                weights[j] = results.tile([P, BATCH, SLOTS], F32, name="weights")
+            neg_max[i] = small.tile([P, HEADS], F32, name="neg_max")
+            sums[i] = small.tile([P, HEADS], F32, name="sums")
+            for half in range(HALVES):
+                nc.vector.tensor_reduce(
+                    out=neg_max[i][:, 2 * half : 2 * half + 2],
+                    in_=scores[(i, half)][:].rearrange("p (h l) -> p h l", l=HEAD),
+                    axis=mybir.AxisListType.X,
+                    op=ALU.max,
+                    negate=True,
+                )
+            for h in range(HEADS):
+                half, side = divmod(h, 2)
+                nc.scalar.activation(
+                    out=weights[j][:, b, h * HEAD : (h + 1) * HEAD],
+                    in_=scores[(i, half)][:, side * HEAD : (side + 1) * HEAD],
+                    func=ACT.Exp,
+                    bias=neg_max[i][:, h : h + 1],
+                    scale=1.0,
+                    accum_out=sums[i][:, h : h + 1],
+                )
+
+        def normalise(i):
+            j, b = divmod(i, BATCH)
+            inverse = small.tile([P, HEADS], F32)
+            nc.vector.reciprocal(out=inverse[:], in_=sums[i][:])
+            for h in range(HEADS):
+                head = weights[j][:, b, h * HEAD : (h + 1) * HEAD]
+                if h < GPSIMD_HEADS:
+                    nc.gpsimd.tensor_scalar(
+                        out=head, in0=head, scalar1=inverse[:, h : h + 1], scalar2=0.0,
+                        op0=ALU.mult, op1=ALU.add,
+                    )
+                else:
+                    nc.vector.tensor_scalar(
+                        out=head, in0=head, scalar1=inverse[:, h : h + 1], scalar2=None,
+                        op0=ALU.mult,
+                    )
+            if b == BATCH - 1:
+                nc.sync.dma_start(out=out_view[:, j, :, :], in_=weights[j][:])
+
+        quantise_queries(0)
+        for half in range(HALVES):
+            quantise_weights(half)
+        quantise_queries(1)
+        multiply(0)
+        multiply(1)
+        for i in range(TILES):
+            j, b = divmod(i, BATCH)
+            if b == 0 and j + 2 < ROUNDS:
+                quantise_queries(j + 2)
+            if i + 2 < TILES:
+                multiply(i + 2)
+            exponentials(i)
+            if i >= 2:
+                normalise(i - 2)
+        normalise(TILES - 2)
+        normalise(TILES - 1)

@@ -24,6 +24,7 @@ ROUNDS = TOKENS // P
 TILES = ROUNDS * BATCH
 WORDS = DEPTH // 2
 GPSIMD_HEADS = 3
+AHEAD = 4
 
 FLOPS = 2 * BATCH * TOKENS * DEPTH * SLOTS
 
@@ -32,9 +33,8 @@ def tile_latentattention_pb_t_kernel(tc, query, wq, out):
     nc = tc.nc
     with ExitStack() as ctx:
         keep = ctx.enter_context(tc.tile_pool(name="keep", bufs=1))
-        stage = ctx.enter_context(tc.tile_pool(name="stage", bufs=3))
         small = ctx.enter_context(tc.tile_pool(name="small", bufs=8))
-        results = ctx.enter_context(tc.tile_pool(name="results", bufs=6))
+        results = ctx.enter_context(tc.tile_pool(name="results", bufs=8))
         psum_t = ctx.enter_context(tc.psum_pool(name="psum_t", bufs=2))
         psum_q = ctx.enter_context(tc.psum_pool(name="psum_q", bufs=6))
 
@@ -42,16 +42,22 @@ def tile_latentattention_pb_t_kernel(tc, query, wq, out):
         out_view = out.rearrange("(p j) b h l -> p j b (h l)", j=ROUNDS)
         wq_view = wq.rearrange("(u q e) c -> q u (e c)", u=2, e=2)
 
-        q_raw = keep.tile([P, BATCH, ROUNDS, DEPTH], BF16)
+        q_words = {}
+
+        def load_queries(first, count):
+            piece = keep.tile([P, BATCH, count, DEPTH], BF16, name="q_raw%d" % first)
+            nc.sync.dma_start(out=piece[:], in_=query_view[:, :, first : first + count, :])
+            for j in range(count):
+                q_words[first + j] = piece[:].bitcast(F32)[:, :, j, :]
+
         w_raw = keep.tile([P, 4, SLOTS], BF16)
-        nc.sync.dma_start(out=q_raw[:, :, 0:1, :], in_=query_view[:, :, 0:1, :])
+        load_queries(0, 1)
         nc.sync.dma_start(out=w_raw[:].rearrange("p (u e) c -> p u (e c)", u=2), in_=wq_view)
-        first = 1
-        for piece in range(4):
-            nc.sync.dma_start(
-                out=q_raw[:, :, first : 2 * first, :], in_=query_view[:, :, first : 2 * first, :]
-            )
-            first = 2 * first
+        loaded = 1
+        for doubling in range(4):
+            load_queries(loaded, loaded)
+            loaded = 2 * loaded
+        assert loaded == ROUNDS
 
         ident = keep.tile([P, P], F32)
         make_identity(nc, ident[:])
@@ -60,36 +66,46 @@ def tile_latentattention_pb_t_kernel(tc, query, wq, out):
         nc.vector.memset(zero[:], 0.0)
         nc.scalar.activation(out=one[:], in_=zero[:], func=ACT.Exp)
 
-        q_words = q_raw[:].bitcast(F32)
+        q_grouped = keep.tile([P, ROUNDS, BATCH, P, 4], BF16, align_bytes=64)
         q_codes = keep.tile([P, ROUNDS, BATCH * P], U32, align_bytes=64)
         q_scales = keep.tile([P, ROUNDS, BATCH * P], U8, align_bytes=64)
         w_grouped = keep.tile([P, SLOTS, 4], BF16, align_bytes=64)
         w_codes = keep.tile([P, SLOTS], U32, align_bytes=64)
         w_scales = keep.tile([P, SLOTS], U8, align_bytes=64)
 
-        def quantise_queries(j):
-            turned = psum_t.tile([P, BATCH, 2, P], F32)
+        turned = {}
+
+        def transpose_queries(j):
+            turned[j] = psum_t.tile([P, BATCH, 2, P], F32, name="turned")
             for b in range(BATCH):
                 for u in range(2):
                     nc.tensor.transpose(
-                        turned[:, b, u, :], q_words[:, b, j, u * P : (u + 1) * P], ident[:]
+                        turned[j][:, b, u, :], q_words[j][:, b, u * P : (u + 1) * P], ident[:]
                     )
-            grouped = stage.tile([P, BATCH, P, 4], BF16, align_bytes=64)
-            nc.scalar.copy(
-                out=grouped[:].bitcast(F32), in_=turned[:].rearrange("p b u r -> p b r u")
-            )
+
+        def group_queries(j):
+            side_by_side = turned[j][:].rearrange("p b u r -> p b r u")
+            if j < AHEAD:
+                nc.scalar.copy(out=q_grouped[:, j].bitcast(F32), in_=side_by_side)
+            else:
+                nc.vector.tensor_copy(out=q_grouped[:, j].bitcast(F32), in_=side_by_side)
+
+        def quantise_queries(j):
             nc.vector.quantize_mx(
                 out=q_codes[:, j, :].bitcast(FP8X4),
                 scales=q_scales[:, j, :],
-                in_=grouped[:].rearrange("p b r t -> p (b r t)"),
+                in_=q_grouped[:, j].rearrange("p b r t -> p (b r t)"),
             )
 
-        def quantise_weights(half):
+        def group_weights(half):
             cols = slice(half * BANK, (half + 1) * BANK)
             nc.vector.tensor_copy(
                 out=w_grouped[:, cols, :].rearrange("p (c i) t -> p c t i", i=4),
                 in_=w_raw[:, :, cols].rearrange("p t (c i) -> p c t i", i=4),
             )
+
+        def quantise_weights(half):
+            cols = slice(half * BANK, (half + 1) * BANK)
             nc.vector.quantize_mx(
                 out=w_codes[:, cols].bitcast(FP8X4),
                 scales=w_scales[:, cols],
@@ -117,12 +133,8 @@ def tile_latentattention_pb_t_kernel(tc, query, wq, out):
                 )
                 scores[(i, half)] = bank
 
-        def exponentials(i):
-            j, b = divmod(i, BATCH)
-            if b == 0:
-                weights[j] = results.tile([P, BATCH, SLOTS], F32, name="weights")
+        def maxima(i):
             neg_max[i] = small.tile([P, HEADS], F32, name="neg_max")
-            sums[i] = small.tile([P, HEADS], F32, name="sums")
             for half in range(HALVES):
                 nc.vector.tensor_reduce(
                     out=neg_max[i][:, 2 * half : 2 * half + 2],
@@ -131,10 +143,14 @@ def tile_latentattention_pb_t_kernel(tc, query, wq, out):
                     op=ALU.max,
                     negate=True,
                 )
+
+        def exponentials(i):
+            weights[i] = results.tile([P, SLOTS], F32, name="weights")
+            sums[i] = small.tile([P, HEADS], F32, name="sums")
             for h in range(HEADS):
                 half, side = divmod(h, 2)
                 nc.scalar.activation(
-                    out=weights[j][:, b, h * HEAD : (h + 1) * HEAD],
+                    out=weights[i][:, h * HEAD : (h + 1) * HEAD],
                     in_=scores[(i, half)][:, side * HEAD : (side + 1) * HEAD],
                     func=ACT.Exp,
                     bias=neg_max[i][:, h : h + 1],
@@ -147,34 +163,45 @@ def tile_latentattention_pb_t_kernel(tc, query, wq, out):
             inverse = small.tile([P, HEADS], F32)
             nc.vector.reciprocal(out=inverse[:], in_=sums[i][:])
             for h in range(HEADS):
-                head = weights[j][:, b, h * HEAD : (h + 1) * HEAD]
+                head = weights[i][:, h * HEAD : (h + 1) * HEAD]
                 if h < GPSIMD_HEADS:
                     nc.gpsimd.tensor_scalar(
                         out=head, in0=head, scalar1=inverse[:, h : h + 1], scalar2=0.0,
                         op0=ALU.mult, op1=ALU.add,
                     )
                 else:
-                    nc.vector.tensor_scalar(
-                        out=head, in0=head, scalar1=inverse[:, h : h + 1], scalar2=None,
-                        op0=ALU.mult,
+                    nc.scalar.activation(
+                        out=head, in_=head, func=ACT.Copy, scale=inverse[:, h : h + 1]
                     )
-            if b == BATCH - 1:
-                nc.sync.dma_start(out=out_view[:, j, :, :], in_=weights[j][:])
+            nc.sync.dma_start(out=out_view[:, j, b, :], in_=weights[i][:])
 
-        quantise_queries(0)
-        for half in range(HALVES):
-            quantise_weights(half)
-        quantise_queries(1)
-        multiply(0)
-        multiply(1)
-        for i in range(TILES):
-            j, b = divmod(i, BATCH)
-            if b == 0 and j + 2 < ROUNDS:
-                quantise_queries(j + 2)
-            if i + 2 < TILES:
-                multiply(i + 2)
-            exponentials(i)
-            if i >= 2:
-                normalise(i - 2)
-        normalise(TILES - 2)
-        normalise(TILES - 1)
+        with tc.manual_schedule():
+            transpose_queries(0)
+            group_queries(0)
+            quantise_queries(0)
+            for half in range(HALVES):
+                group_weights(half)
+            for half in range(HALVES):
+                quantise_weights(half)
+            for j in range(1, AHEAD):
+                transpose_queries(j)
+                group_queries(j)
+            quantise_queries(1)
+            multiply(0)
+            multiply(1)
+            for i in range(TILES):
+                j, b = divmod(i, BATCH)
+                if b == 0 and j + AHEAD < ROUNDS:
+                    transpose_queries(j + AHEAD)
+                if i + 2 < TILES:
+                    multiply(i + 2)
+                maxima(i)
+                exponentials(i)
+                if b == 0 and j + AHEAD < ROUNDS:
+                    group_queries(j + AHEAD)
+                if b == 1 and j + 2 < ROUNDS:
+                    quantise_queries(j + 2)
+                if i >= 2:
+                    normalise(i - 2)
+            normalise(TILES - 2)
+            normalise(TILES - 1)

@@ -23,7 +23,8 @@ HALVES = SLOTS // BANK
 ROUNDS = TOKENS // P
 TILES = ROUNDS * BATCH
 WORDS = DEPTH // 2
-GPSIMD_HEADS = 3
+GPSIMD_HEADS_EARLY = 3
+GPSIMD_HEADS_LATE = 2
 AHEAD = 4
 
 FLOPS = 2 * BATCH * TOKENS * DEPTH * SLOTS
@@ -40,7 +41,7 @@ def tile_latentattention_pb_t_kernel(tc, query, wq, out):
 
         query_view = query.rearrange("b (p j) d -> p b j d", j=ROUNDS)
         out_view = out.rearrange("(p j) b h l -> p j b (h l)", j=ROUNDS)
-        wq_view = wq.rearrange("(u q e) c -> q u (e c)", u=2, e=2)
+        wq_view = wq.rearrange("(u q e) c -> u q e c", u=2, e=2)
 
         q_words = {}
 
@@ -50,9 +51,14 @@ def tile_latentattention_pb_t_kernel(tc, query, wq, out):
             for j in range(count):
                 q_words[first + j] = piece[:].bitcast(F32)[:, :, j, :]
 
-        w_raw = keep.tile([P, 4, SLOTS], BF16)
+        w_raw = [keep.tile([P, 4, BANK], BF16, name="w_raw%d" % half) for half in range(HALVES)]
         load_queries(0, 1)
-        nc.sync.dma_start(out=w_raw[:].rearrange("p (u e) c -> p u (e c)", u=2), in_=wq_view)
+        for half in range(HALVES):
+            for u in range(2):
+                nc.sync.dma_start(
+                    out=w_raw[half][:, 2 * u : 2 * u + 2, :],
+                    in_=wq_view[u, :, :, half * BANK : (half + 1) * BANK],
+                )
         loaded = 1
         for doubling in range(4):
             load_queries(loaded, loaded)
@@ -101,7 +107,7 @@ def tile_latentattention_pb_t_kernel(tc, query, wq, out):
             cols = slice(half * BANK, (half + 1) * BANK)
             nc.vector.tensor_copy(
                 out=w_grouped[:, cols, :].rearrange("p (c i) t -> p c t i", i=4),
-                in_=w_raw[:, :, cols].rearrange("p t (c i) -> p c t i", i=4),
+                in_=w_raw[half][:].rearrange("p t (c i) -> p c t i", i=4),
             )
 
         def quantise_weights(half):
@@ -162,12 +168,18 @@ def tile_latentattention_pb_t_kernel(tc, query, wq, out):
             j, b = divmod(i, BATCH)
             inverse = small.tile([P, HEADS], F32)
             nc.vector.reciprocal(out=inverse[:], in_=sums[i][:])
+            early = j + AHEAD < ROUNDS
             for h in range(HEADS):
                 head = weights[i][:, h * HEAD : (h + 1) * HEAD]
-                if h < GPSIMD_HEADS:
+                if h < (GPSIMD_HEADS_EARLY if early else GPSIMD_HEADS_LATE):
                     nc.gpsimd.tensor_scalar(
                         out=head, in0=head, scalar1=inverse[:, h : h + 1], scalar2=0.0,
                         op0=ALU.mult, op1=ALU.add,
+                    )
+                elif not early:
+                    nc.vector.tensor_scalar(
+                        out=head, in0=head, scalar1=inverse[:, h : h + 1], scalar2=None,
+                        op0=ALU.mult,
                     )
                 else:
                     nc.scalar.activation(
@@ -201,7 +213,6 @@ def tile_latentattention_pb_t_kernel(tc, query, wq, out):
                     group_queries(j + AHEAD)
                 if b == 1 and j + 2 < ROUNDS:
                     quantise_queries(j + 2)
-                if i >= 2:
-                    normalise(i - 2)
-            normalise(TILES - 2)
+                if i >= 1:
+                    normalise(i - 1)
             normalise(TILES - 1)

@@ -168,15 +168,15 @@ def tile_latentattention_pb_t_kernel(tc, query, wq, out):
             j, b = divmod(i, BATCH)
             inverse = small.tile([P, HEADS], F32)
             nc.vector.reciprocal(out=inverse[:], in_=sums[i][:])
-            early = j + AHEAD < ROUNDS
+            gpsimd_heads = GPSIMD_HEADS_EARLY if j + AHEAD < ROUNDS else GPSIMD_HEADS_LATE
             for h in range(HEADS):
                 head = weights[i][:, h * HEAD : (h + 1) * HEAD]
-                if h < (GPSIMD_HEADS_EARLY if early else GPSIMD_HEADS_LATE):
+                if h < gpsimd_heads:
                     nc.gpsimd.tensor_scalar(
                         out=head, in0=head, scalar1=inverse[:, h : h + 1], scalar2=0.0,
                         op0=ALU.mult, op1=ALU.add,
                     )
-                elif not early:
+                elif h < HEADS - 1:
                     nc.vector.tensor_scalar(
                         out=head, in0=head, scalar1=inverse[:, h : h + 1], scalar2=None,
                         op0=ALU.mult,

from contextlib import ExitStack

import concourse.mybir as mybir
from concourse.masks import make_identity

F32 = mybir.dt.float32
BF16 = mybir.dt.bfloat16
U32 = mybir.dt.uint32
U8 = mybir.dt.uint8
FP8X4 = mybir.dt.float8_e4m3fn_x4
ALU = mybir.AluOpType
ACT = mybir.ActivationFunctionType

P = 128
BATCH = 2
TOKENS = 2048
DEPTH = 512
SLOTS = 1024
HEADS = 4
HEAD = SLOTS // HEADS
BANK = 512
HALVES = SLOTS // BANK
ROUNDS = TOKENS // P
TILES = ROUNDS * BATCH
WORDS = DEPTH // 2
GPSIMD_HEADS_EARLY = 3
GPSIMD_HEADS_LATE = 2
AHEAD = 4

FLOPS = 2 * BATCH * TOKENS * DEPTH * SLOTS


def tile_latentattention_pb_t_kernel(tc, query, wq, out):
    nc = tc.nc
    with ExitStack() as ctx:
        keep = ctx.enter_context(tc.tile_pool(name="keep", bufs=1))
        small = ctx.enter_context(tc.tile_pool(name="small", bufs=8))
        results = ctx.enter_context(tc.tile_pool(name="results", bufs=8))
        psum_t = ctx.enter_context(tc.psum_pool(name="psum_t", bufs=2))
        psum_q = ctx.enter_context(tc.psum_pool(name="psum_q", bufs=6))

        query_view = query.rearrange("b (p j) d -> p b j d", j=ROUNDS)
        out_view = out.rearrange("(p j) b h l -> p j b (h l)", j=ROUNDS)
        wq_view = wq.rearrange("(u q e) c -> u q e c", u=2, e=2)

        q_words = {}

        def load_queries(first, count):
            piece = keep.tile([P, BATCH, count, DEPTH], BF16, name="q_raw%d" % first)
            nc.sync.dma_start(out=piece[:], in_=query_view[:, :, first : first + count, :])
            for j in range(count):
                q_words[first + j] = piece[:].bitcast(F32)[:, :, j, :]

        w_raw = [keep.tile([P, 4, BANK], BF16, name="w_raw%d" % half) for half in range(HALVES)]
        load_queries(0, 1)
        for half in range(HALVES):
            for u in range(2):
                nc.sync.dma_start(
                    out=w_raw[half][:, 2 * u : 2 * u + 2, :],
                    in_=wq_view[u, :, :, half * BANK : (half + 1) * BANK],
                )
        loaded = 1
        for doubling in range(4):
            load_queries(loaded, loaded)
            loaded = 2 * loaded
        assert loaded == ROUNDS

        ident = keep.tile([P, P], F32)
        make_identity(nc, ident[:])
        zero = keep.tile([P, 1], F32)
        one = keep.tile([P, 1], F32)
        nc.vector.memset(zero[:], 0.0)
        nc.scalar.activation(out=one[:], in_=zero[:], func=ACT.Exp)

        q_grouped = keep.tile([P, ROUNDS, BATCH, P, 4], BF16, align_bytes=64)
        q_codes = keep.tile([P, ROUNDS, BATCH * P], U32, align_bytes=64)
        q_scales = keep.tile([P, ROUNDS, BATCH * P], U8, align_bytes=64)
        w_grouped = keep.tile([P, SLOTS, 4], BF16, align_bytes=64)
        w_codes = keep.tile([P, SLOTS], U32, align_bytes=64)
        w_scales = keep.tile([P, SLOTS], U8, align_bytes=64)

        turned = {}

        def transpose_queries(j):
            turned[j] = psum_t.tile([P, BATCH, 2, P], F32, name="turned")
            for b in range(BATCH):
                for u in range(2):
                    nc.tensor.transpose(
                        turned[j][:, b, u, :], q_words[j][:, b, u * P : (u + 1) * P], ident[:]
                    )

        def group_queries(j):
            side_by_side = turned[j][:].rearrange("p b u r -> p b r u")
            if j < AHEAD:
                nc.scalar.copy(out=q_grouped[:, j].bitcast(F32), in_=side_by_side)
            else:
                nc.vector.tensor_copy(out=q_grouped[:, j].bitcast(F32), in_=side_by_side)

        def quantise_queries(j):
            nc.vector.quantize_mx(
                out=q_codes[:, j, :].bitcast(FP8X4),
                scales=q_scales[:, j, :],
                in_=q_grouped[:, j].rearrange("p b r t -> p (b r t)"),
            )

        def group_weights(half):
            cols = slice(half * BANK, (half + 1) * BANK)
            nc.vector.tensor_copy(
                out=w_grouped[:, cols, :].rearrange("p (c i) t -> p c t i", i=4),
                in_=w_raw[half][:].rearrange("p t (c i) -> p c t i", i=4),
            )

        def quantise_weights(half):
            cols = slice(half * BANK, (half + 1) * BANK)
            nc.vector.quantize_mx(
                out=w_codes[:, cols].bitcast(FP8X4),
                scales=w_scales[:, cols],
                in_=w_grouped[:, cols, :].rearrange("p c t -> p (c t)"),
            )

        scores = {}
        neg_max = {}
        sums = {}
        weights = {}

        def multiply(i):
            j, b = divmod(i, BATCH)
            for half in range(HALVES):
                cols = slice(half * BANK, (half + 1) * BANK)
                bank = psum_q.tile([P, BANK], F32, name="bank")
                nc.tensor.matmul_mx(
                    out=bank[:],
                    lhsT=q_codes[:, j, b * P : (b + 1) * P].bitcast(FP8X4),
                    lhsT_scale=q_scales[:, j, b * P : (b + 1) * P],
                    rhs=w_codes[:, cols].bitcast(FP8X4),
                    rhs_scale=w_scales[:, cols],
                    start=True,
                    stop=True,
                )
                scores[(i, half)] = bank

        def maxima(i):
            neg_max[i] = small.tile([P, HEADS], F32, name="neg_max")
            for half in range(HALVES):
                nc.vector.tensor_reduce(
                    out=neg_max[i][:, 2 * half : 2 * half + 2],
                    in_=scores[(i, half)][:].rearrange("p (h l) -> p h l", l=HEAD),
                    axis=mybir.AxisListType.X,
                    op=ALU.max,
                    negate=True,
                )

        def exponentials(i):
            weights[i] = results.tile([P, SLOTS], F32, name="weights")
            sums[i] = small.tile([P, HEADS], F32, name="sums")
            for h in range(HEADS):
                half, side = divmod(h, 2)
                nc.scalar.activation(
                    out=weights[i][:, h * HEAD : (h + 1) * HEAD],
                    in_=scores[(i, half)][:, side * HEAD : (side + 1) * HEAD],
                    func=ACT.Exp,
                    bias=neg_max[i][:, h : h + 1],
                    scale=1.0,
                    accum_out=sums[i][:, h : h + 1],
                )

        def normalise(i):
            j, b = divmod(i, BATCH)
            inverse = small.tile([P, HEADS], F32)
            nc.vector.reciprocal(out=inverse[:], in_=sums[i][:])
            gpsimd_heads = GPSIMD_HEADS_EARLY if j + AHEAD < ROUNDS else GPSIMD_HEADS_LATE
            for h in range(HEADS):
                head = weights[i][:, h * HEAD : (h + 1) * HEAD]
                if h < gpsimd_heads:
                    nc.gpsimd.tensor_scalar(
                        out=head, in0=head, scalar1=inverse[:, h : h + 1], scalar2=0.0,
                        op0=ALU.mult, op1=ALU.add,
                    )
                elif h < HEADS - 1:
                    nc.vector.tensor_scalar(
                        out=head, in0=head, scalar1=inverse[:, h : h + 1], scalar2=None,
                        op0=ALU.mult,
                    )
                else:
                    nc.scalar.activation(
                        out=head, in_=head, func=ACT.Copy, scale=inverse[:, h : h + 1]
                    )
            nc.sync.dma_start(out=out_view[:, j, b, :], in_=weights[i][:])

        with tc.manual_schedule():
            transpose_queries(0)
            group_queries(0)
            quantise_queries(0)
            for half in range(HALVES):
                group_weights(half)
            for half in range(HALVES):
                quantise_weights(half)
            for j in range(1, AHEAD):
                transpose_queries(j)
                group_queries(j)
            quantise_queries(1)
            multiply(0)
            multiply(1)
            for i in range(TILES):
                j, b = divmod(i, BATCH)
                if b == 0 and j + AHEAD < ROUNDS:
                    transpose_queries(j + AHEAD)
                if i + 2 < TILES:
                    multiply(i + 2)
                maxima(i)
                exponentials(i)
                if b == 0 and j + AHEAD < ROUNDS:
                    group_queries(j + AHEAD)
                if b == 1 and j + 2 < ROUNDS:
                    quantise_queries(j + 2)
                if i >= 1:
                    normalise(i - 1)
            normalise(TILES - 1)
